import numpy as np
import ml_dtypes


def mxq(x, axis, fmt="e4m3"):
    dtype, down = {"e4m3": (ml_dtypes.float8_e4m3fn, 7), "e5m2": (ml_dtypes.float8_e5m2, 14)}[fmt]
    v = np.moveaxis(np.asarray(x, np.float32).astype(ml_dtypes.bfloat16).astype(np.float64), axis, -1)
    blocks = v.reshape(v.shape[:-1] + (-1, 32))
    amax = np.abs(blocks).max(-1, keepdims=True)
    byte = np.maximum(np.where(amax > 0, np.frexp(amax)[1] - 1 + 127, 0) - down, 1)
    scale = np.exp2(byte - 127.0)
    codes = (blocks / scale).astype(np.float32).astype(dtype).astype(np.float64)
    return np.moveaxis((codes * scale).reshape(v.shape), -1, axis)


WIDE = False


def mx_kscale(k):
    if not WIDE:
        return np.ones(k)
    levels = np.array([10, -10, 5, -5, 0])
    a = np.random.permutation(np.resize(levels, k // 512 * 4)).reshape(k // 512, 4)
    idx = np.arange(k)
    return np.exp2(a[idx // 512, idx % 128 // 32])


BF16 = ml_dtypes.bfloat16


def bf(x):
    return np.asarray(x, np.float32).astype(BF16)


def f64(x):
    return np.asarray(x).astype(np.float64)


B, D = 2048, 1024


def setup_inputs():
    s = mx_kscale(D)
    return {"x": bf(np.random.standard_normal((B, D)) * s),
            "W": bf(np.random.standard_normal((D, D)) * 0.04 / s[None, :]),
            "b": bf(np.random.standard_normal(D) * 0.5)}


def reference(x, W, b):
    d = W.shape[0]
    mask = np.tril(np.ones((d, d), dtype=np.float64), k=-1)
    wm = f64(W) * mask
    return (mxq(f64(x), 1, "e4m3") @ mxq(wm, 1, "e4m3").T) + f64(b)

@@ -1,0 +1,203 @@
+from contextlib import ExitStack
+
+import concourse.mybir as mybir
+from concourse.masks import make_identity
+
+F32 = mybir.dt.float32
+BF16 = mybir.dt.bfloat16
+U32 = mybir.dt.uint32
+U8 = mybir.dt.uint8
+FP8X4 = mybir.dt.float8_e4m3fn_x4
+ALU = mybir.AluOpType
+
+P = 128
+B = 2048
+D = 1024
+HALF = 512
+N_TILES = B // P
+GROUP = 2
+PINNED = True
+N_GROUPS = N_TILES // GROUP
+
+FLOPS = 2 * B * (D * (D - 1) // 2)
+BYTES = 2 * B * D + 2 * (D * (D - 1) // 2) + 2 * D + 4 * B * D
+
+
+def tile_fvsbn_kernel(tc, x, W, b, out):
+    nc = tc.nc
+    with ExitStack() as ctx:
+        const = ctx.enter_context(tc.tile_pool(name="const", bufs=1))
+        wpool = ctx.enter_context(tc.tile_pool(name="wpool", bufs=1))
+        xpool = ctx.enter_context(tc.tile_pool(name="xpool", bufs=1))
+        opool = ctx.enter_context(tc.tile_pool(name="opool", bufs=1))
+        psum_t = ctx.enter_context(tc.psum_pool(name="psum_t", bufs=2))
+        psum_o = ctx.enter_context(tc.psum_pool(name="psum_o", bufs=6))
+        if PINNED:
+            ctx.enter_context(tc.manual_schedule())
+
+        maskf = const.tile([P, 2, 256], F32, name="maskf")
+        nc.vector.memset(maskf[:], 1.0)
+        zeros = const.tile([P, P], F32, name="zeros")
+        nc.vector.memset(zeros[:], 0.0)
+        brow = const.tile([P, D], BF16, name="brow")
+        nc.vector.memset(brow[:], 0.0)
+        ones = const.tile([P, P], BF16, name="ones")
+        nc.vector.memset(ones[:], 1.0)
+        ident = const.tile([P, P], F32, name="ident")
+        make_identity(nc, ident[:])
+        for s in range(2):
+            nc.gpsimd.affine_select(
+                out=maskf[:, s, :],
+                in_=maskf[:, s, :],
+                pattern=[[-1, 256]],
+                compare_op=ALU.is_gt,
+                fill=0.0,
+                base=P * s,
+                channel_multiplier=1,
+            )
+        maskb = const.tile([P, 2, 256], BF16, name="maskb")
+        nc.vector.tensor_copy(out=maskb[:], in_=maskf[:])
+        bias = const.tile([P, D], F32, name="bias")
+
+        nc.scalar.dma_start(out=brow[0:1, :], in_=b.rearrange("(o n) -> o n", o=1))
+        w_sb = []
+        for j in range(4):
+            width = 256 * (j + 1)
+            w_t = wpool.tile([P, 2, width], BF16, name="w%d" % j)
+            nc.sync.dma_start(
+                out=w_t[:],
+                in_=W[256 * j : 256 * (j + 1), 0:width].rearrange("(s p) d -> p s d", p=P),
+            )
+            w_sb.append(w_t)
+        x_sb = []
+        for q in range(N_GROUPS):
+            x_t = xpool.tile([P, GROUP, D], BF16, name="x%d" % q)
+            rows = x[q * GROUP * P : (q + 1) * GROUP * P, :]
+            nc.sync.dma_start(out=x_t[:], in_=rows.rearrange("(p t) d -> p t d", t=GROUP))
+            x_sb.append(x_t)
+
+        w_codes = {}
+        w_scales = {}
+        for key in ((0, 0), (1, 0), (1, 1)):
+            w_codes[key] = wpool.tile([P, HALF], U32, name="wc%d%d" % key, align_bytes=64)
+            w_scales[key] = wpool.tile([P, HALF], U8, name="ws%d%d" % key, align_bytes=64)
+        w_grouped = {}
+        x_grouped = []
+        x_codes = []
+        x_scales = []
+        o_sb = []
+        for q in range(N_GROUPS):
+            x_grouped.append(xpool.tile([P, GROUP * D], BF16, name="xg%d" % q, align_bytes=64))
+            x_codes.append(xpool.tile([P, GROUP * D // 4], U32, name="xc%d" % q, align_bytes=64))
+            x_scales.append(xpool.tile([P, GROUP * D // 4], U8, name="xs%d" % q, align_bytes=64))
+            o_sb.append(opool.tile([P, GROUP, D], F32, name="o%d" % q))
+
+        def flip(blocks, grouped_words):
+            bank = psum_t.tile([P, 4, P], F32, name="bank")
+            for i, block in blocks:
+                nc.tensor.transpose(bank[:, i, :], block, ident[:])
+            nc.scalar.copy(
+                out=grouped_words.rearrange("p (a r u) -> p a r u", a=2, u=2),
+                in_=bank[:].rearrange("p (a u) r -> p a r u", u=2),
+            )
+
+        def mask_w(j):
+            diag = w_sb[j][:, :, 256 * j : 256 * (j + 1)]
+            nc.vector.tensor_tensor(out=diag, in0=diag, in1=maskb[:], op=ALU.mult)
+
+        def flip_w(j, g):
+            words = w_sb[j][:].bitcast(F32)
+            blocks = []
+            for u in (1, 0):
+                c = 2 * g + u
+                for s in range(2):
+                    if c <= j:
+                        blocks.append((2 * s + u, words[:, s, P * c : P * (c + 1)]))
+                    else:
+                        blocks.append((2 * s + u, zeros[:]))
+            grouped = wpool.tile([P, D], BF16, name="wg%d%d" % (j, g), align_bytes=64)
+            w_grouped[(j, g)] = grouped
+            flip(blocks, grouped[:].bitcast(F32))
+
+        def quant_w(j, g):
+            key = (j // 2, g)
+            cols = slice(256 * (j % 2), 256 * (j % 2 + 1))
+            nc.vector.quantize_mx(
+                out=w_codes[key][:, cols].bitcast(FP8X4),
+                scales=w_scales[key][:, cols],
+                in_=w_grouped[(j, g)][:],
+            )
+
+        def make_bias():
+            for h in range(2):
+                cols = slice(HALF * h, HALF * (h + 1))
+                acc = psum_o.tile([P, HALF], F32, name="acc")
+                nc.tensor.matmul(acc[:], lhsT=ones[:], rhs=brow[:, cols], start=True, stop=True)
+                nc.scalar.copy(out=bias[:, cols], in_=acc[:])
+
+        def flip_x(t):
+            q, a = divmod(t, GROUP)
+            words = x_sb[q][:].bitcast(F32)
+            blocks = [(c, words[:, a, P * c : P * (c + 1)]) for c in range(4)]
+            flip(blocks, x_grouped[q][:].bitcast(F32)[:, HALF * a : HALF * (a + 1)])
+
+        def quant_x(q):
+            nc.vector.quantize_mx(
+                out=x_codes[q][:].bitcast(FP8X4), scales=x_scales[q][:], in_=x_grouped[q][:]
+            )
+
+        def product(t, h):
+            q, a = divmod(t, GROUP)
+            acc = psum_o.tile([P, HALF], F32, name="acc")
+            for g in range(h + 1):
+                rows = slice(P * (2 * a + g), P * (2 * a + g + 1))
+                nc.tensor.matmul_mx(
+                    out=acc[:],
+                    lhsT=x_codes[q][:, rows].bitcast(FP8X4),
+                    lhsT_scale=x_scales[q][:, rows],
+                    rhs=w_codes[(h, g)][:].bitcast(FP8X4),
+                    rhs_scale=w_scales[(h, g)][:],
+                    start=(g == 0),
+                    stop=(g == h),
+                )
+            cols = slice(HALF * h, HALF * (h + 1))
+            nc.vector.tensor_tensor(out=o_sb[q][:, a, cols], in0=acc[:], in1=bias[:, cols], op=ALU.add)
+
+        def store(t):
+            q, a = divmod(t, GROUP)
+            rows = out[q * GROUP * P : (q + 1) * GROUP * P, :]
+            nc.sync.dma_start(
+                out=rows.rearrange("(p t) n -> p t n", t=GROUP)[:, a, :], in_=o_sb[q][:, a, :]
+            )
+
+        mask_w(0)
+        flip_w(0, 0)
+        mask_w(1)
+        flip_w(1, 0)
+        mask_w(2)
+        quant_w(0, 0)
+        flip_w(2, 0)
+        quant_w(1, 0)
+        flip_w(2, 1)
+        mask_w(3)
+        flip_w(3, 0)
+        quant_w(2, 0)
+        quant_w(2, 1)
+        flip_w(3, 1)
+        quant_w(3, 0)
+        flip_x(0)
+        quant_w(3, 1)
+        flip_x(1)
+        make_bias()
+        quant_x(0)
+        for q in range(N_GROUPS):
+            if q + 1 < N_GROUPS:
+                for a in range(GROUP):
+                    flip_x((q + 1) * GROUP + a)
+            for a in range(GROUP):
+                t = q * GROUP + a
+                product(t, 0)
+                product(t, 1)
+                store(t)
+                if a == 0 and q + 1 < N_GROUPS:
+                    quant_x(q + 1)

@@ -17,6 +17,9 @@ HALF = 512
 N_TILES = B // P
 GROUP = 2
 PINNED = True
+WARM_FIRST = 4
+WARM_EACH = 1
+OFFLOAD_BELOW = 0
 N_GROUPS = N_TILES // GROUP
 
 FLOPS = 2 * B * (D * (D - 1) // 2)
@@ -37,12 +40,12 @@ def tile_fvsbn_kernel(tc, x, W, b, out):
 
         maskf = const.tile([P, 2, 256], F32, name="maskf")
         nc.vector.memset(maskf[:], 1.0)
-        zeros = const.tile([P, P], F32, name="zeros")
+        zeros = const.tile([P, 2 * P], F32, name="zeros")
         nc.vector.memset(zeros[:], 0.0)
-        brow = const.tile([P, D], BF16, name="brow")
-        nc.vector.memset(brow[:], 0.0)
         ones = const.tile([P, P], BF16, name="ones")
         nc.vector.memset(ones[:], 1.0)
+        brow = const.tile([P, D], BF16, name="brow")
+        nc.vector.memset(brow[:], 0.0)
         ident = const.tile([P, P], F32, name="ident")
         make_identity(nc, ident[:])
         for s in range(2):
@@ -101,6 +104,14 @@ def tile_fvsbn_kernel(tc, x, W, b, out):
                 in_=bank[:].rearrange("p (a u) r -> p a r u", u=2),
             )
 
+        warm_bank = psum_o.tile([P, HALF], F32, name="acc")
+
+        def warm(count):
+            for i in range(count):
+                nc.tensor.matmul(
+                    warm_bank[:], lhsT=ones[:], rhs=zeros[:].bitcast(BF16), start=True, stop=True
+                )
+
         def mask_w(j):
             diag = w_sb[j][:, :, 256 * j : 256 * (j + 1)]
             nc.vector.tensor_tensor(out=diag, in0=diag, in1=maskb[:], op=ALU.mult)
@@ -114,7 +125,7 @@ def tile_fvsbn_kernel(tc, x, W, b, out):
                     if c <= j:
                         blocks.append((2 * s + u, words[:, s, P * c : P * (c + 1)]))
                     else:
-                        blocks.append((2 * s + u, zeros[:]))
+                        blocks.append((2 * s + u, zeros[:, 0:P]))
             grouped = wpool.tile([P, D], BF16, name="wg%d%d" % (j, g), align_bytes=64)
             w_grouped[(j, g)] = grouped
             flip(blocks, grouped[:].bitcast(F32))
@@ -161,7 +172,12 @@ def tile_fvsbn_kernel(tc, x, W, b, out):
                     stop=(g == h),
                 )
             cols = slice(HALF * h, HALF * (h + 1))
-            nc.vector.tensor_tensor(out=o_sb[q][:, a, cols], in0=acc[:], in1=bias[:, cols], op=ALU.add)
+            dest = o_sb[q][:, a, cols]
+            if h == 0 and a == 0 and t < OFFLOAD_BELOW:
+                nc.scalar.copy(out=dest, in_=acc[:])
+                nc.gpsimd.tensor_tensor(out=dest, in0=dest, in1=bias[:, cols], op=ALU.add)
+            else:
+                nc.vector.tensor_tensor(out=dest, in0=acc[:], in1=bias[:, cols], op=ALU.add)
 
         def store(t):
             q, a = divmod(t, GROUP)
@@ -170,20 +186,27 @@ def tile_fvsbn_kernel(tc, x, W, b, out):
                 out=rows.rearrange("(p t) n -> p t n", t=GROUP)[:, a, :], in_=o_sb[q][:, a, :]
             )
 
+        warm(WARM_FIRST)
         mask_w(0)
         flip_w(0, 0)
+        warm(WARM_EACH)
         mask_w(1)
         flip_w(1, 0)
+        warm(WARM_EACH)
         mask_w(2)
         quant_w(0, 0)
         flip_w(2, 0)
+        warm(WARM_EACH)
         quant_w(1, 0)
         flip_w(2, 1)
+        warm(WARM_EACH)
         mask_w(3)
         flip_w(3, 0)
+        warm(WARM_EACH)
         quant_w(2, 0)
         quant_w(2, 1)
         flip_w(3, 1)
+        warm(WARM_EACH)
         quant_w(3, 0)
         flip_x(0)
         quant_w(3, 1)

@@ -19,7 +19,7 @@ GROUP = 2
 PINNED = True
 WARM_FIRST = 4
 WARM_EACH = 1
-OFFLOAD_BELOW = 0
+OFFLOAD_BELOW = 12
 N_GROUPS = N_TILES // GROUP
 
 FLOPS = 2 * B * (D * (D - 1) // 2)

@@ -33,8 +33,8 @@ def tile_fvsbn_kernel(tc, x, W, b, out):
         wpool = ctx.enter_context(tc.tile_pool(name="wpool", bufs=1))
         xpool = ctx.enter_context(tc.tile_pool(name="xpool", bufs=1))
         opool = ctx.enter_context(tc.tile_pool(name="opool", bufs=1))
-        psum_t = ctx.enter_context(tc.psum_pool(name="psum_t", bufs=2))
-        psum_o = ctx.enter_context(tc.psum_pool(name="psum_o", bufs=6))
+        psum_t = ctx.enter_context(tc.psum_pool(name="psum_t", bufs=3))
+        psum_o = ctx.enter_context(tc.psum_pool(name="psum_o", bufs=5))
         if PINNED:
             ctx.enter_context(tc.manual_schedule())
 
@@ -95,14 +95,16 @@ def tile_fvsbn_kernel(tc, x, W, b, out):
             x_scales.append(xpool.tile([P, GROUP * D // 4], U8, name="xs%d" % q, align_bytes=64))
             o_sb.append(opool.tile([P, GROUP, D], F32, name="o%d" % q))
 
-        def flip(blocks, grouped_words):
+        def flip(blocks, grouped_words, on_vector=False):
             bank = psum_t.tile([P, 4, P], F32, name="bank")
             for i, block in blocks:
                 nc.tensor.transpose(bank[:, i, :], block, ident[:])
-            nc.scalar.copy(
-                out=grouped_words.rearrange("p (a r u) -> p a r u", a=2, u=2),
-                in_=bank[:].rearrange("p (a u) r -> p a r u", u=2),
-            )
+            dest = grouped_words.rearrange("p (a r u) -> p a r u", a=2, u=2)
+            source = bank[:].rearrange("p (a u) r -> p a r u", u=2)
+            if on_vector:
+                nc.vector.tensor_copy(out=dest, in_=source)
+            else:
+                nc.scalar.copy(out=dest, in_=source)
 
         warm_bank = psum_o.tile([P, HALF], F32, name="acc")
 
@@ -116,7 +118,7 @@ def tile_fvsbn_kernel(tc, x, W, b, out):
             diag = w_sb[j][:, :, 256 * j : 256 * (j + 1)]
             nc.vector.tensor_tensor(out=diag, in0=diag, in1=maskb[:], op=ALU.mult)
 
-        def flip_w(j, g):
+        def flip_w(j, g, on_vector=False):
             words = w_sb[j][:].bitcast(F32)
             blocks = []
             for u in (1, 0):
@@ -128,7 +130,7 @@ def tile_fvsbn_kernel(tc, x, W, b, out):
                         blocks.append((2 * s + u, zeros[:, 0:P]))
             grouped = wpool.tile([P, D], BF16, name="wg%d%d" % (j, g), align_bytes=64)
             w_grouped[(j, g)] = grouped
-            flip(blocks, grouped[:].bitcast(F32))
+            flip(blocks, grouped[:].bitcast(F32), on_vector)
 
         def quant_w(j, g):
             key = (j // 2, g)
@@ -144,7 +146,7 @@ def tile_fvsbn_kernel(tc, x, W, b, out):
                 cols = slice(HALF * h, HALF * (h + 1))
                 acc = psum_o.tile([P, HALF], F32, name="acc")
                 nc.tensor.matmul(acc[:], lhsT=ones[:], rhs=brow[:, cols], start=True, stop=True)
-                nc.scalar.copy(out=bias[:, cols], in_=acc[:])
+                nc.vector.tensor_copy(out=bias[:, cols], in_=acc[:])
 
         def flip_x(t):
             q, a = divmod(t, GROUP)
@@ -152,9 +154,12 @@ def tile_fvsbn_kernel(tc, x, W, b, out):
             blocks = [(c, words[:, a, P * c : P * (c + 1)]) for c in range(4)]
             flip(blocks, x_grouped[q][:].bitcast(F32)[:, HALF * a : HALF * (a + 1)])
 
-        def quant_x(q):
+        def quant_x(q, first=0, count=GROUP):
+            words = slice(first * D // 4, (first + count) * D // 4)
             nc.vector.quantize_mx(
-                out=x_codes[q][:].bitcast(FP8X4), scales=x_scales[q][:], in_=x_grouped[q][:]
+                out=x_codes[q][:, words].bitcast(FP8X4),
+                scales=x_scales[q][:, words],
+                in_=x_grouped[q][:, first * D : (first + count) * D],
             )
 
         def product(t, h):
@@ -202,17 +207,16 @@ def tile_fvsbn_kernel(tc, x, W, b, out):
         warm(WARM_EACH)
         mask_w(3)
         flip_w(3, 0)
-        warm(WARM_EACH)
         quant_w(2, 0)
         quant_w(2, 1)
-        flip_w(3, 1)
-        warm(WARM_EACH)
+        flip_w(3, 1, on_vector=True)
         quant_w(3, 0)
         flip_x(0)
         quant_w(3, 1)
+        quant_x(0, 0, 1)
         flip_x(1)
+        quant_x(0, 1, 1)
         make_bias()
-        quant_x(0)
         for q in range(N_GROUPS):
             if q + 1 < N_GROUPS:
                 for a in range(GROUP):

@@ -17,7 +17,7 @@ HALF = 512
 N_TILES = B // P
 GROUP = 2
 PINNED = True
-WARM_FIRST = 4
+WARM_FIRST = 6
 WARM_EACH = 1
 OFFLOAD_BELOW = 12
 N_GROUPS = N_TILES // GROUP
@@ -141,12 +141,19 @@ def tile_fvsbn_kernel(tc, x, W, b, out):
                 in_=w_grouped[(j, g)][:],
             )
 
-        def make_bias():
+        bias_banks = []
+
+        def bias_products():
             for h in range(2):
-                cols = slice(HALF * h, HALF * (h + 1))
                 acc = psum_o.tile([P, HALF], F32, name="acc")
-                nc.tensor.matmul(acc[:], lhsT=ones[:], rhs=brow[:, cols], start=True, stop=True)
-                nc.vector.tensor_copy(out=bias[:, cols], in_=acc[:])
+                nc.tensor.matmul(
+                    acc[:], lhsT=ones[:], rhs=brow[:, HALF * h : HALF * (h + 1)], start=True, stop=True
+                )
+                bias_banks.append(acc)
+
+        def bias_copies():
+            for h in range(2):
+                nc.vector.tensor_copy(out=bias[:, HALF * h : HALF * (h + 1)], in_=bias_banks[h][:])
 
         def flip_x(t):
             q, a = divmod(t, GROUP)
@@ -212,19 +219,22 @@ def tile_fvsbn_kernel(tc, x, W, b, out):
         flip_w(3, 1, on_vector=True)
         quant_w(3, 0)
         flip_x(0)
+        bias_products()
         quant_w(3, 1)
         quant_x(0, 0, 1)
         flip_x(1)
         quant_x(0, 1, 1)
-        make_bias()
+        bias_copies()
         for q in range(N_GROUPS):
             if q + 1 < N_GROUPS:
                 for a in range(GROUP):
                     flip_x((q + 1) * GROUP + a)
+            if q == 0:
+                quant_x(1)
             for a in range(GROUP):
                 t = q * GROUP + a
                 product(t, 0)
                 product(t, 1)
                 store(t)
-                if a == 0 and q + 1 < N_GROUPS:
+                if a == 0 and 0 < q < N_GROUPS - 1:
                     quant_x(q + 1)

@@ -17,7 +17,7 @@ HALF = 512
 N_TILES = B // P
 GROUP = 2
 PINNED = True
-WARM_FIRST = 6
+WARM_FIRST = 4
 WARM_EACH = 1
 OFFLOAD_BELOW = 12
 N_GROUPS = N_TILES // GROUP
@@ -141,19 +141,12 @@ def tile_fvsbn_kernel(tc, x, W, b, out):
                 in_=w_grouped[(j, g)][:],
             )
 
-        bias_banks = []
-
-        def bias_products():
+        def make_bias():
             for h in range(2):
+                cols = slice(HALF * h, HALF * (h + 1))
                 acc = psum_o.tile([P, HALF], F32, name="acc")
-                nc.tensor.matmul(
-                    acc[:], lhsT=ones[:], rhs=brow[:, HALF * h : HALF * (h + 1)], start=True, stop=True
-                )
-                bias_banks.append(acc)
-
-        def bias_copies():
-            for h in range(2):
-                nc.vector.tensor_copy(out=bias[:, HALF * h : HALF * (h + 1)], in_=bias_banks[h][:])
+                nc.tensor.matmul(acc[:], lhsT=ones[:], rhs=brow[:, cols], start=True, stop=True)
+                nc.vector.tensor_copy(out=bias[:, cols], in_=acc[:])
 
         def flip_x(t):
             q, a = divmod(t, GROUP)
@@ -217,24 +210,23 @@ def tile_fvsbn_kernel(tc, x, W, b, out):
         quant_w(2, 0)
         quant_w(2, 1)
         flip_w(3, 1, on_vector=True)
+        warm(WARM_EACH)
         quant_w(3, 0)
         flip_x(0)
-        bias_products()
+        warm(WARM_EACH)
         quant_w(3, 1)
         quant_x(0, 0, 1)
         flip_x(1)
         quant_x(0, 1, 1)
-        bias_copies()
+        make_bias()
         for q in range(N_GROUPS):
             if q + 1 < N_GROUPS:
                 for a in range(GROUP):
                     flip_x((q + 1) * GROUP + a)
-            if q == 0:
-                quant_x(1)
             for a in range(GROUP):
                 t = q * GROUP + a
                 product(t, 0)
                 product(t, 1)
                 store(t)
-                if a == 0 and 0 < q < N_GROUPS - 1:
+                if a == 0 and q + 1 < N_GROUPS:
                     quant_x(q + 1)

@@ -33,8 +33,8 @@ def tile_fvsbn_kernel(tc, x, W, b, out):
         wpool = ctx.enter_context(tc.tile_pool(name="wpool", bufs=1))
         xpool = ctx.enter_context(tc.tile_pool(name="xpool", bufs=1))
         opool = ctx.enter_context(tc.tile_pool(name="opool", bufs=1))
-        psum_t = ctx.enter_context(tc.psum_pool(name="psum_t", bufs=3))
-        psum_o = ctx.enter_context(tc.psum_pool(name="psum_o", bufs=5))
+        psum_t = ctx.enter_context(tc.psum_pool(name="psum_t", bufs=2))
+        psum_o = ctx.enter_context(tc.psum_pool(name="psum_o", bufs=6))
         if PINNED:
             ctx.enter_context(tc.manual_schedule())
 
@@ -95,16 +95,14 @@ def tile_fvsbn_kernel(tc, x, W, b, out):
             x_scales.append(xpool.tile([P, GROUP * D // 4], U8, name="xs%d" % q, align_bytes=64))
             o_sb.append(opool.tile([P, GROUP, D], F32, name="o%d" % q))
 
-        def flip(blocks, grouped_words, on_vector=False):
+        def flip(blocks, grouped_words):
             bank = psum_t.tile([P, 4, P], F32, name="bank")
             for i, block in blocks:
                 nc.tensor.transpose(bank[:, i, :], block, ident[:])
-            dest = grouped_words.rearrange("p (a r u) -> p a r u", a=2, u=2)
-            source = bank[:].rearrange("p (a u) r -> p a r u", u=2)
-            if on_vector:
-                nc.vector.tensor_copy(out=dest, in_=source)
-            else:
-                nc.scalar.copy(out=dest, in_=source)
+            nc.scalar.copy(
+                out=grouped_words.rearrange("p (a r u) -> p a r u", a=2, u=2),
+                in_=bank[:].rearrange("p (a u) r -> p a r u", u=2),
+            )
 
         warm_bank = psum_o.tile([P, HALF], F32, name="acc")
 
@@ -118,7 +116,7 @@ def tile_fvsbn_kernel(tc, x, W, b, out):
             diag = w_sb[j][:, :, 256 * j : 256 * (j + 1)]
             nc.vector.tensor_tensor(out=diag, in0=diag, in1=maskb[:], op=ALU.mult)
 
-        def flip_w(j, g, on_vector=False):
+        def flip_w(j, g):
             words = w_sb[j][:].bitcast(F32)
             blocks = []
             for u in (1, 0):
@@ -130,7 +128,7 @@ def tile_fvsbn_kernel(tc, x, W, b, out):
                         blocks.append((2 * s + u, zeros[:, 0:P]))
             grouped = wpool.tile([P, D], BF16, name="wg%d%d" % (j, g), align_bytes=64)
             w_grouped[(j, g)] = grouped
-            flip(blocks, grouped[:].bitcast(F32), on_vector)
+            flip(blocks, grouped[:].bitcast(F32))
 
         def quant_w(j, g):
             key = (j // 2, g)
@@ -146,7 +144,7 @@ def tile_fvsbn_kernel(tc, x, W, b, out):
                 cols = slice(HALF * h, HALF * (h + 1))
                 acc = psum_o.tile([P, HALF], F32, name="acc")
                 nc.tensor.matmul(acc[:], lhsT=ones[:], rhs=brow[:, cols], start=True, stop=True)
-                nc.vector.tensor_copy(out=bias[:, cols], in_=acc[:])
+                nc.scalar.copy(out=bias[:, cols], in_=acc[:])
 
         def flip_x(t):
             q, a = divmod(t, GROUP)
@@ -207,18 +205,18 @@ def tile_fvsbn_kernel(tc, x, W, b, out):
         warm(WARM_EACH)
         mask_w(3)
         flip_w(3, 0)
+        warm(WARM_EACH)
         quant_w(2, 0)
         quant_w(2, 1)
-        flip_w(3, 1, on_vector=True)
+        flip_w(3, 1)
         warm(WARM_EACH)
         quant_w(3, 0)
         flip_x(0)
-        warm(WARM_EACH)
         quant_w(3, 1)
-        quant_x(0, 0, 1)
         flip_x(1)
-        quant_x(0, 1, 1)
+        quant_x(0, 0, 1)
         make_bias()
+        quant_x(0, 1, 1)
         for q in range(N_GROUPS):
             if q + 1 < N_GROUPS:
                 for a in range(GROUP):

@@ -16,6 +16,7 @@ D = 1024
 HALF = 512
 N_TILES = B // P
 GROUP = 2
+PAD = 48
 PINNED = True
 WARM_FIRST = 4
 WARM_EACH = 1
@@ -82,8 +83,8 @@ def tile_fvsbn_kernel(tc, x, W, b, out):
         w_codes = {}
         w_scales = {}
         for key in ((0, 0), (1, 0), (1, 1)):
-            w_codes[key] = wpool.tile([P, HALF], U32, name="wc%d%d" % key, align_bytes=64)
-            w_scales[key] = wpool.tile([P, HALF], U8, name="ws%d%d" % key, align_bytes=64)
+            w_codes[key] = wpool.tile([P, HALF], U32, name="wc%d%d" % key, align_bytes=256)
+            w_scales[key] = wpool.tile([P, HALF], U8, name="ws%d%d" % key, align_bytes=256)
         w_grouped = {}
         x_grouped = []
         x_codes = []
@@ -91,8 +92,8 @@ def tile_fvsbn_kernel(tc, x, W, b, out):
         o_sb = []
         for q in range(N_GROUPS):
             x_grouped.append(xpool.tile([P, GROUP * D], BF16, name="xg%d" % q, align_bytes=64))
-            x_codes.append(xpool.tile([P, GROUP * D // 4], U32, name="xc%d" % q, align_bytes=64))
-            x_scales.append(xpool.tile([P, GROUP * D // 4], U8, name="xs%d" % q, align_bytes=64))
+            x_codes.append(xpool.tile([P, PAD + GROUP * D // 4], U32, name="xc%d" % q, align_bytes=256))
+            x_scales.append(xpool.tile([P, GROUP * D // 4], U8, name="xs%d" % q, align_bytes=256))
             o_sb.append(opool.tile([P, GROUP, D], F32, name="o%d" % q))
 
         def flip(blocks, grouped_words):
@@ -155,7 +156,7 @@ def tile_fvsbn_kernel(tc, x, W, b, out):
         def quant_x(q, first=0, count=GROUP):
             words = slice(first * D // 4, (first + count) * D // 4)
             nc.vector.quantize_mx(
-                out=x_codes[q][:, words].bitcast(FP8X4),
+                out=x_codes[q][:, PAD + first * D // 4 : PAD + (first + count) * D // 4].bitcast(FP8X4),
                 scales=x_scales[q][:, words],
                 in_=x_grouped[q][:, first * D : (first + count) * D],
             )
@@ -167,7 +168,7 @@ def tile_fvsbn_kernel(tc, x, W, b, out):
                 rows = slice(P * (2 * a + g), P * (2 * a + g + 1))
                 nc.tensor.matmul_mx(
                     out=acc[:],
-                    lhsT=x_codes[q][:, rows].bitcast(FP8X4),
+                    lhsT=x_codes[q][:, PAD + P * (2 * a + g) : PAD + P * (2 * a + g + 1)].bitcast(FP8X4),
                     lhsT_scale=x_scales[q][:, rows],
                     rhs=w_codes[(h, g)][:].bitcast(FP8X4),
                     rhs_scale=w_scales[(h, g)][:],

from contextlib import ExitStack

import concourse.mybir as mybir
from concourse.masks import make_identity

F32 = mybir.dt.float32
BF16 = mybir.dt.bfloat16
U32 = mybir.dt.uint32
U8 = mybir.dt.uint8
FP8X4 = mybir.dt.float8_e4m3fn_x4
ALU = mybir.AluOpType

P = 128
B = 2048
D = 1024
HALF = 512
N_TILES = B // P
GROUP = 2
PAD = 48
PINNED = True
WARM_FIRST = 4
WARM_EACH = 1
OFFLOAD_BELOW = 12
N_GROUPS = N_TILES // GROUP

FLOPS = 2 * B * (D * (D - 1) // 2)
BYTES = 2 * B * D + 2 * (D * (D - 1) // 2) + 2 * D + 4 * B * D


def tile_fvsbn_kernel(tc, x, W, b, out):
    nc = tc.nc
    with ExitStack() as ctx:
        const = ctx.enter_context(tc.tile_pool(name="const", bufs=1))
        wpool = ctx.enter_context(tc.tile_pool(name="wpool", bufs=1))
        xpool = ctx.enter_context(tc.tile_pool(name="xpool", bufs=1))
        opool = ctx.enter_context(tc.tile_pool(name="opool", bufs=1))
        psum_t = ctx.enter_context(tc.psum_pool(name="psum_t", bufs=2))
        psum_o = ctx.enter_context(tc.psum_pool(name="psum_o", bufs=6))
        if PINNED:
            ctx.enter_context(tc.manual_schedule())

        maskf = const.tile([P, 2, 256], F32, name="maskf")
        nc.vector.memset(maskf[:], 1.0)
        zeros = const.tile([P, 2 * P], F32, name="zeros")
        nc.vector.memset(zeros[:], 0.0)
        ones = const.tile([P, P], BF16, name="ones")
        nc.vector.memset(ones[:], 1.0)
        brow = const.tile([P, D], BF16, name="brow")
        nc.vector.memset(brow[:], 0.0)
        ident = const.tile([P, P], F32, name="ident")
        make_identity(nc, ident[:])
        for s in range(2):
            nc.gpsimd.affine_select(
                out=maskf[:, s, :],
                in_=maskf[:, s, :],
                pattern=[[-1, 256]],
                compare_op=ALU.is_gt,
                fill=0.0,
                base=P * s,
                channel_multiplier=1,
            )
        maskb = const.tile([P, 2, 256], BF16, name="maskb")
        nc.vector.tensor_copy(out=maskb[:], in_=maskf[:])
        bias = const.tile([P, D], F32, name="bias")

        nc.scalar.dma_start(out=brow[0:1, :], in_=b.rearrange("(o n) -> o n", o=1))
        w_sb = []
        for j in range(4):
            width = 256 * (j + 1)
            w_t = wpool.tile([P, 2, width], BF16, name="w%d" % j)
            nc.sync.dma_start(
                out=w_t[:],
                in_=W[256 * j : 256 * (j + 1), 0:width].rearrange("(s p) d -> p s d", p=P),
            )
            w_sb.append(w_t)
        x_sb = []
        for q in range(N_GROUPS):
            x_t = xpool.tile([P, GROUP, D], BF16, name="x%d" % q)
            rows = x[q * GROUP * P : (q + 1) * GROUP * P, :]
            nc.sync.dma_start(out=x_t[:], in_=rows.rearrange("(p t) d -> p t d", t=GROUP))
            x_sb.append(x_t)

        w_codes = {}
        w_scales = {}
        for key in ((0, 0), (1, 0), (1, 1)):
            w_codes[key] = wpool.tile([P, HALF], U32, name="wc%d%d" % key, align_bytes=256)
            w_scales[key] = wpool.tile([P, HALF], U8, name="ws%d%d" % key, align_bytes=256)
        w_grouped = {}
        x_grouped = []
        x_codes = []
        x_scales = []
        o_sb = []
        for q in range(N_GROUPS):
            x_grouped.append(xpool.tile([P, GROUP * D], BF16, name="xg%d" % q, align_bytes=64))
            x_codes.append(xpool.tile([P, PAD + GROUP * D // 4], U32, name="xc%d" % q, align_bytes=256))
            x_scales.append(xpool.tile([P, GROUP * D // 4], U8, name="xs%d" % q, align_bytes=256))
            o_sb.append(opool.tile([P, GROUP, D], F32, name="o%d" % q))

        def flip(blocks, grouped_words):
            bank = psum_t.tile([P, 4, P], F32, name="bank")
            for i, block in blocks:
                nc.tensor.transpose(bank[:, i, :], block, ident[:])
            nc.scalar.copy(
                out=grouped_words.rearrange("p (a r u) -> p a r u", a=2, u=2),
                in_=bank[:].rearrange("p (a u) r -> p a r u", u=2),
            )

        warm_bank = psum_o.tile([P, HALF], F32, name="acc")

        def warm(count):
            for i in range(count):
                nc.tensor.matmul(
                    warm_bank[:], lhsT=ones[:], rhs=zeros[:].bitcast(BF16), start=True, stop=True
                )

        def mask_w(j):
            diag = w_sb[j][:, :, 256 * j : 256 * (j + 1)]
            nc.vector.tensor_tensor(out=diag, in0=diag, in1=maskb[:], op=ALU.mult)

        def flip_w(j, g):
            words = w_sb[j][:].bitcast(F32)
            blocks = []
            for u in (1, 0):
                c = 2 * g + u
                for s in range(2):
                    if c <= j:
                        blocks.append((2 * s + u, words[:, s, P * c : P * (c + 1)]))
                    else:
                        blocks.append((2 * s + u, zeros[:, 0:P]))
            grouped = wpool.tile([P, D], BF16, name="wg%d%d" % (j, g), align_bytes=64)
            w_grouped[(j, g)] = grouped
            flip(blocks, grouped[:].bitcast(F32))

        def quant_w(j, g):
            key = (j // 2, g)
            cols = slice(256 * (j % 2), 256 * (j % 2 + 1))
            nc.vector.quantize_mx(
                out=w_codes[key][:, cols].bitcast(FP8X4),
                scales=w_scales[key][:, cols],
                in_=w_grouped[(j, g)][:],
            )

        def make_bias():
            for h in range(2):
                cols = slice(HALF * h, HALF * (h + 1))
                acc = psum_o.tile([P, HALF], F32, name="acc")
                nc.tensor.matmul(acc[:], lhsT=ones[:], rhs=brow[:, cols], start=True, stop=True)
                nc.scalar.copy(out=bias[:, cols], in_=acc[:])

        def flip_x(t):
            q, a = divmod(t, GROUP)
            words = x_sb[q][:].bitcast(F32)
            blocks = [(c, words[:, a, P * c : P * (c + 1)]) for c in range(4)]
            flip(blocks, x_grouped[q][:].bitcast(F32)[:, HALF * a : HALF * (a + 1)])

        def quant_x(q, first=0, count=GROUP):
            words = slice(first * D // 4, (first + count) * D // 4)
            nc.vector.quantize_mx(
                out=x_codes[q][:, PAD + first * D // 4 : PAD + (first + count) * D // 4].bitcast(FP8X4),
                scales=x_scales[q][:, words],
                in_=x_grouped[q][:, first * D : (first + count) * D],
            )

        def product(t, h):
            q, a = divmod(t, GROUP)
            acc = psum_o.tile([P, HALF], F32, name="acc")
            for g in range(h + 1):
                rows = slice(P * (2 * a + g), P * (2 * a + g + 1))
                nc.tensor.matmul_mx(
                    out=acc[:],
                    lhsT=x_codes[q][:, PAD + P * (2 * a + g) : PAD + P * (2 * a + g + 1)].bitcast(FP8X4),
                    lhsT_scale=x_scales[q][:, rows],
                    rhs=w_codes[(h, g)][:].bitcast(FP8X4),
                    rhs_scale=w_scales[(h, g)][:],
                    start=(g == 0),
                    stop=(g == h),
                )
            cols = slice(HALF * h, HALF * (h + 1))
            dest = o_sb[q][:, a, cols]
            if h == 0 and a == 0 and t < OFFLOAD_BELOW:
                nc.scalar.copy(out=dest, in_=acc[:])
                nc.gpsimd.tensor_tensor(out=dest, in0=dest, in1=bias[:, cols], op=ALU.add)
            else:
                nc.vector.tensor_tensor(out=dest, in0=acc[:], in1=bias[:, cols], op=ALU.add)

        def store(t):
            q, a = divmod(t, GROUP)
            rows = out[q * GROUP * P : (q + 1) * GROUP * P, :]
            nc.sync.dma_start(
                out=rows.rearrange("(p t) n -> p t n", t=GROUP)[:, a, :], in_=o_sb[q][:, a, :]
            )

        warm(WARM_FIRST)
        mask_w(0)
        flip_w(0, 0)
        warm(WARM_EACH)
        mask_w(1)
        flip_w(1, 0)
        warm(WARM_EACH)
        mask_w(2)
        quant_w(0, 0)
        flip_w(2, 0)
        warm(WARM_EACH)
        quant_w(1, 0)
        flip_w(2, 1)
        warm(WARM_EACH)
        mask_w(3)
        flip_w(3, 0)
        warm(WARM_EACH)
        quant_w(2, 0)
        quant_w(2, 1)
        flip_w(3, 1)
        warm(WARM_EACH)
        quant_w(3, 0)
        flip_x(0)
        quant_w(3, 1)
        flip_x(1)
        quant_x(0, 0, 1)
        make_bias()
        quant_x(0, 1, 1)
        for q in range(N_GROUPS):
            if q + 1 < N_GROUPS:
                for a in range(GROUP):
                    flip_x((q + 1) * GROUP + a)
            for a in range(GROUP):
                t = q * GROUP + a
                product(t, 0)
                product(t, 1)
                store(t)
                if a == 0 and q + 1 < N_GROUPS:
                    quant_x(q + 1)
